import numpy as np
import ml_dtypes


def mxq(x, axis, fmt="e4m3"):
    dtype, down = {"e4m3": (ml_dtypes.float8_e4m3fn, 7), "e5m2": (ml_dtypes.float8_e5m2, 14)}[fmt]
    v = np.moveaxis(np.asarray(x, np.float32).astype(ml_dtypes.bfloat16).astype(np.float64), axis, -1)
    blocks = v.reshape(v.shape[:-1] + (-1, 32))
    amax = np.abs(blocks).max(-1, keepdims=True)
    byte = np.maximum(np.where(amax > 0, np.frexp(amax)[1] - 1 + 127, 0) - down, 1)
    scale = np.exp2(byte - 127.0)
    codes = (blocks / scale).astype(np.float32).astype(dtype).astype(np.float64)
    return np.moveaxis((codes * scale).reshape(v.shape), -1, axis)


WIDE = False


def mx_kscale(k):
    if not WIDE:
        return np.ones(k)
    levels = np.array([10, -10, 5, -5, 0])
    if k % 512:
        return np.exp2(np.random.permutation(np.resize(levels, k // 32))).repeat(32)
    a = np.empty((k // 512, 16))
    for p in range(k // 512):
        a[p, :8] = np.random.permutation(np.resize(levels, 8))
        for g in range(8):
            far = levels[np.abs(levels - a[p, g]) >= 10]
            a[p, g + 8] = far[np.random.randint(len(far))]
    return np.exp2(a.ravel()).repeat(32)


BF16 = ml_dtypes.bfloat16


def bf(x):
    return np.asarray(x, np.float32).astype(BF16)


def f64(x):
    return np.asarray(x).astype(np.float64)


B, U, I, O = 128, 8, 512, 256


def sigmoid(v):
    return 1.0 / (1.0 + np.exp(-v))


def draw0():
    s = mx_kscale(I)
    wi = lambda: bf(np.random.standard_normal((U, I, O)) / np.sqrt(I) / s[None, :, None])
    wh = lambda: bf(np.random.standard_normal((U, O, O)) / np.sqrt(O))
    return {"x": bf(np.random.standard_normal((B, U, I)) * s),
            "h": bf(np.random.standard_normal((B, U, O))),
            "w_ir": wi(), "w_iz": wi(), "w_in": wi(),
            "w_hr": wh(), "w_hz": wh(), "w_hn": wh()}


def core(x, h, w_ir, w_iz, w_in, w_hr, w_hz, w_hn):
    xq = mxq(f64(x).transpose(1, 0, 2), 2, "e4m3")
    hu = f64(h).transpose(1, 0, 2)
    r = sigmoid((xq @ mxq(f64(w_ir), 1, "e4m3")) + hu @ f64(w_hr))
    z = sigmoid((xq @ mxq(f64(w_iz), 1, "e4m3")) + hu @ f64(w_hz))
    n = np.tanh((xq @ mxq(f64(w_in), 1, "e4m3")) + r * (hu @ f64(w_hn)))
    return ((1.0 - z) * n + z * hu).transpose(1, 0, 2)


def e4m3fn_bytes(y):
    return np.clip(np.asarray(y, np.float64), -448.0, 448.0).astype(np.float32).astype(ml_dtypes.float8_e4m3fn).view(np.uint8)


def e4m3fn_values(b):
    return np.asarray(b, np.uint8).view(ml_dtypes.float8_e4m3fn).astype(np.float64)


def setup_inputs():
    d = draw0()
    x0 = np.asarray(d['w_iz']).astype(np.float64)
    s = (np.max(np.abs(x0), axis=(0, 2), keepdims=True) / 448.0).astype(np.float32)
    out = {}
    for k, v in d.items():
        if k == 'w_iz':
            out['w_iz_bytes'] = e4m3fn_bytes(x0 / s.astype(np.float64))
            out['w_iz_scale'] = s
        else:
            out[k] = v
    return out


def reference(x, h, w_ir, w_iz_bytes, w_iz_scale, w_in, w_hr, w_hz, w_hn):
    return core(x, h, w_ir, e4m3fn_values(w_iz_bytes) * w_iz_scale.astype(np.float64), w_in, w_hr, w_hz, w_hn)

@@ -1,0 +1,202 @@
+from contextlib import ExitStack
+
+import concourse.mybir as mybir
+from concourse.masks import make_identity
+
+B, U, I, O = 128, 8, 512, 256
+FLOPS = 2 * B * U * O * 3 * (I + O)
+
+F32 = mybir.dt.float32
+BF16 = mybir.dt.bfloat16
+U32 = mybir.dt.uint32
+U8 = mybir.dt.uint8
+FP8 = mybir.dt.float8_e4m3fn
+FP8X4 = mybir.dt.float8_e4m3fn_x4
+ACT = mybir.ActivationFunctionType
+ALU = mybir.AluOpType
+
+P = 128
+PACK = 4
+PAIRS = U // 2
+AHEAD = 2
+
+
+def tile_unitwisegru_pa_kernel(tc, x, h, w_ir, w_iz_bytes, w_iz_scale, w_in, w_hr, w_hz, w_hn, out):
+    nc = tc.nc
+    with ExitStack() as ctx:
+        const = ctx.enter_context(tc.tile_pool(name="const", bufs=1))
+        loads = ctx.enter_context(tc.tile_pool(name="loads", bufs=1))
+        work = ctx.enter_context(tc.tile_pool(name="work", bufs=4))
+        epi = ctx.enter_context(tc.tile_pool(name="epi", bufs=3))
+        psum = ctx.enter_context(tc.psum_pool(name="psum", bufs=2))
+
+        x_sb, h_sb, wr_raw, wn_raw, wz_bytes, whr, whz, whn = [], [], [], [], [], [], [], []
+        scl = const.tile([P, PACK], F32, name="scl")
+
+        def load_pair_small(q):
+            xt = loads.tile([P, 2 * I], BF16, name="x%d" % q)
+            nc.sync.dma_start(out=xt[:], in_=x[:, 2 * q : 2 * q + 2, :].rearrange("b u i -> b (u i)"))
+            x_sb.append(xt)
+            ht = loads.tile([P, 2 * O], BF16, name="h%d" % q)
+            nc.sync.dma_start(out=ht[:], in_=h[:, 2 * q : 2 * q + 2, :].rearrange("b u o -> b (u o)"))
+            h_sb.append(ht)
+
+        def load_unit(u, src, lst, nm):
+            t = loads.tile([P, PACK, O], BF16, name="%s%d" % (nm, u))
+            nc.sync.dma_start(out=t[:], in_=src[u].rearrange("(p t) c -> p t c", t=PACK))
+            lst.append(t)
+
+        def load_bytes(q):
+            t = loads.tile([P, 2, PACK * O], U8, name="wzb%d" % q)
+            nc.sync.dma_start(out=t[:], in_=w_iz_bytes[2 * q : 2 * q + 2].rearrange("u (p t) c -> p u (t c)", t=PACK))
+            wz_bytes.append(t)
+
+        def load_hidden(q, src, lst, nm):
+            t = loads.tile([P, 2, 2 * O], BF16, name="%s%d" % (nm, q))
+            nc.sync.dma_start(out=t[:], in_=src[2 * q : 2 * q + 2].rearrange("u (p e) c -> p u (e c)", e=2))
+            lst.append(t)
+
+        for q in range(PAIRS):
+            load_unit(2 * q, w_ir, wr_raw, "wr")
+            if q == 0:
+                nc.sync.dma_start(out=scl[:], in_=w_iz_scale.rearrange("o (p t) q -> p (o t q)", t=PACK))
+            load_pair_small(q)
+            load_bytes(q)
+            load_unit(2 * q, w_in, wn_raw, "wn")
+            load_hidden(q, w_hr, whr, "whr")
+            load_hidden(q, w_hz, whz, "whz")
+            load_hidden(q, w_hn, whn, "whn")
+            load_unit(2 * q + 1, w_ir, wr_raw, "wr")
+            load_unit(2 * q + 1, w_in, wn_raw, "wn")
+
+        ident_f = const.tile([P, P], F32, name="ident_f")
+        make_identity(nc, ident_f[:])
+        ident_b = const.tile([P, P], BF16, name="ident_b")
+        make_identity(nc, ident_b[:])
+        warm_in = const.tile([P, 1], F32, name="warm_in")
+        warm_out = const.tile([P, 1], F32, name="warm_out")
+        nc.vector.memset(warm_in[:], 0.0)
+        nc.scalar.activation(out=warm_out[:], in_=warm_in[:], func=ACT.Sigmoid)
+
+        x_codes, x_scales, h_T = [], [], []
+        codes, scales = {}, {}
+
+        def pair_prep(q):
+            words = x_sb[q][:].bitcast(F32)
+            xt_ps = psum.tile([P, 4 * P], F32, name="xt_ps", tag="tp")
+            for v in range(2):
+                for s in range(2):
+                    nc.tensor.transpose(
+                        xt_ps[:, (2 * v + s) * P : (2 * v + s + 1) * P],
+                        words[:, 256 * v + s : 256 * (v + 1) : 2],
+                        ident_f[:],
+                    )
+            x_grp = work.tile([P, 2 * P * PACK], BF16, name="x_grp", tag="x_grp", align_bytes=64)
+            nc.scalar.copy(
+                out=x_grp[:].bitcast(F32).rearrange("p (v r s) -> p v r s", v=2, s=2),
+                in_=xt_ps[:].rearrange("p (v s r) -> p v r s", v=2, s=2),
+            )
+            ht_ps = psum.tile([P, 4 * P], BF16, name="ht_ps", tag="tp")
+            for v in range(2):
+                for e in range(2):
+                    nc.tensor.transpose(
+                        ht_ps[:, (2 * v + e) * P : (2 * v + e + 1) * P],
+                        h_sb[q][:, O * v + e : O * (v + 1) : 2],
+                        ident_b[:],
+                    )
+            hT = loads.tile([P, 4 * P], BF16, name="hT%d" % q)
+            nc.scalar.copy(out=hT[:], in_=ht_ps[:])
+            h_T.append(hT)
+            xc = loads.tile([P, 2 * P], U32, name="xc%d" % q, align_bytes=64)
+            xs = loads.tile([P, 2 * P], U8, name="xs%d" % q, align_bytes=64)
+            nc.vector.quantize_mx(out=xc[:].bitcast(FP8X4), scales=xs[:], in_=x_grp[:])
+            x_codes.append(xc)
+            x_scales.append(xs)
+
+        def prep(u):
+            q, v = u // 2, u % 2
+            grp = work.tile([P, 3 * PACK * O], BF16, name="grp", tag="grp", align_bytes=64)
+            wz_bf = work.tile([P, PACK, O], BF16, name="wz_bf", tag="wz_bf")
+            for t in range(PACK):
+                nc.scalar.activation(
+                    out=wz_bf[:, t, :],
+                    in_=wz_bytes[q][:, v, t * O : (t + 1) * O].bitcast(FP8),
+                    func=ACT.Copy,
+                    scale=scl[:, t : t + 1],
+                )
+
+            def part(g):
+                return grp[:, g * PACK * O : (g + 1) * PACK * O].rearrange("p (c t) -> p c t", t=PACK)
+
+            nc.vector.tensor_copy(out=part(0), in_=wr_raw[u][:].rearrange("p t c -> p c t"))
+            nc.scalar.copy(out=part(1), in_=wz_bf[:].rearrange("p t c -> p c t"))
+            nc.vector.tensor_copy(out=part(2), in_=wn_raw[u][:].rearrange("p t c -> p c t"))
+            cd = work.tile([P, 3 * O], U32, name="cd", tag="cd", align_bytes=64)
+            sc = work.tile([P, 3 * O], U8, name="sc", tag="sc", align_bytes=64)
+            nc.vector.quantize_mx(
+                out=cd[:, 0 : 2 * O].bitcast(FP8X4), scales=sc[:, 0 : 2 * O], in_=grp[:, 0 : 2 * PACK * O]
+            )
+            nc.vector.quantize_mx(
+                out=cd[:, 2 * O : 3 * O].bitcast(FP8X4), scales=sc[:, 2 * O : 3 * O], in_=grp[:, 2 * PACK * O : 3 * PACK * O]
+            )
+            codes[u] = cd
+            scales[u] = sc
+
+        def unit(u):
+            q, v = u // 2, u % 2
+            rzh_ps = psum.tile([P, 2 * O], F32, name="rzh_ps", tag="rzh")
+            nn_ps = psum.tile([P, 2 * O], F32, name="nn_ps", tag="nn")
+            for dst, wt in ((rzh_ps[:, 0:O], whr), (rzh_ps[:, O : 2 * O], whz), (nn_ps[:, O : 2 * O], whn)):
+                for e in range(2):
+                    nc.tensor.matmul(
+                        out=dst,
+                        lhsT=h_T[q][:, (2 * v + e) * P : (2 * v + e + 1) * P],
+                        rhs=wt[q][:, v, e * O : (e + 1) * O],
+                        start=(e == 0),
+                        stop=(e == 1),
+                    )
+            hs = epi.tile([P, 2 * O], F32, name="hs", tag="hs")
+            nc.scalar.copy(out=hs[:], in_=rzh_ps[:])
+            rzx_ps = psum.tile([P, 2 * O], F32, name="rzx_ps", tag="rzx")
+            xl = x_codes[q][:, v * P : (v + 1) * P].bitcast(FP8X4)
+            xls = x_scales[q][:, v * P : (v + 1) * P]
+            nc.tensor.matmul_mx(
+                out=rzx_ps[:], lhsT=xl, lhsT_scale=xls,
+                rhs=codes[u][:, 0 : 2 * O].bitcast(FP8X4), rhs_scale=scales[u][:, 0 : 2 * O],
+                start=True, stop=True,
+            )
+            nc.tensor.matmul_mx(
+                out=nn_ps[:, 0:O], lhsT=xl, lhsT_scale=xls,
+                rhs=codes[u][:, 2 * O : 3 * O].bitcast(FP8X4), rhs_scale=scales[u][:, 2 * O : 3 * O],
+                start=True, stop=True,
+            )
+            pre = epi.tile([P, 2 * O], F32, name="pre", tag="pre")
+            nc.vector.tensor_tensor(out=pre[:], in0=rzx_ps[:], in1=hs[:], op=ALU.add)
+            rz = epi.tile([P, 2 * O], F32, name="rz", tag="rz")
+            nc.scalar.activation(out=rz[:], in_=pre[:], func=ACT.Sigmoid)
+            rh = epi.tile([P, O], F32, name="rh", tag="rh")
+            nc.vector.tensor_tensor(out=rh[:], in0=nn_ps[:, O : 2 * O], in1=rz[:, 0:O], op=ALU.mult)
+            npre = epi.tile([P, O], F32, name="npre", tag="npre")
+            nc.vector.tensor_tensor(out=npre[:], in0=nn_ps[:, 0:O], in1=rh[:], op=ALU.add)
+            zp = epi.tile([P, O], F32, name="zp", tag="zp")
+            nc.vector.tensor_tensor(out=zp[:], in0=rz[:, O : 2 * O], in1=h_sb[q][:, v * O : (v + 1) * O], op=ALU.mult)
+            nt = epi.tile([P, O], F32, name="nt", tag="nt")
+            nc.scalar.activation(out=nt[:], in_=npre[:], func=ACT.Tanh)
+            zn = epi.tile([P, O], F32, name="zn", tag="zn")
+            nc.vector.scalar_tensor_tensor(
+                out=zn[:], in0=rz[:, O : 2 * O], scalar=1.0, in1=nt[:], op0=ALU.subtract, op1=ALU.mult
+            )
+            res = epi.tile([P, O], F32, name="res", tag="res")
+            nc.vector.tensor_tensor(out=res[:], in0=zp[:], in1=zn[:], op=ALU.subtract)
+            nc.sync.dma_start(out=out[:, u, :], in_=res[:])
+
+        pair_prep(0)
+        for u in range(AHEAD):
+            prep(u)
+        for u in range(U):
+            nxt = u + AHEAD
+            if nxt < U and nxt % 2 == 0:
+                pair_prep(nxt // 2)
+            unit(u)
+            if nxt < U:
+                prep(nxt)

@@ -18,7 +18,7 @@ ALU = mybir.AluOpType
 P = 128
 PACK = 4
 PAIRS = U // 2
-AHEAD = 2
+W = PACK * O
 
 
 def tile_unitwisegru_pa_kernel(tc, x, h, w_ir, w_iz_bytes, w_iz_scale, w_in, w_hr, w_hz, w_hn, out):
@@ -26,48 +26,48 @@ def tile_unitwisegru_pa_kernel(tc, x, h, w_ir, w_iz_bytes, w_iz_scale, w_in, w_h
     with ExitStack() as ctx:
         const = ctx.enter_context(tc.tile_pool(name="const", bufs=1))
         loads = ctx.enter_context(tc.tile_pool(name="loads", bufs=1))
-        work = ctx.enter_context(tc.tile_pool(name="work", bufs=4))
+        work = ctx.enter_context(tc.tile_pool(name="work", bufs=2))
         epi = ctx.enter_context(tc.tile_pool(name="epi", bufs=3))
         psum = ctx.enter_context(tc.psum_pool(name="psum", bufs=2))
 
-        x_sb, h_sb, wr_raw, wn_raw, wz_bytes, whr, whz, whn = [], [], [], [], [], [], [], []
+        x_sb, h_sb, wr_raw, wn_raw, wz_bytes, whr, whz, whn = {}, {}, {}, {}, {}, {}, {}, {}
         scl = const.tile([P, PACK], F32, name="scl")
 
-        def load_pair_small(q):
+        def load_input_weights(q, src, store, nm):
+            t = loads.tile([P, 2, W], BF16, name="%s%d" % (nm, q))
+            for v in range(2):
+                nc.sync.dma_start(out=t[:, v, :], in_=src[2 * q + v].rearrange("(p t) c -> p (t c)", t=PACK))
+            store[q] = t
+
+        def load_prep(q):
+            zb = loads.tile([P, PACK, 2, O], U8, name="wzb%d" % q)
+            for v in range(2):
+                nc.sync.dma_start(out=zb[:, :, v, :], in_=w_iz_bytes[2 * q + v].rearrange("(p t) c -> p t c", t=PACK))
+            wz_bytes[q] = zb
+            load_input_weights(q, w_ir, wr_raw, "wr")
             xt = loads.tile([P, 2 * I], BF16, name="x%d" % q)
             nc.sync.dma_start(out=xt[:], in_=x[:, 2 * q : 2 * q + 2, :].rearrange("b u i -> b (u i)"))
-            x_sb.append(xt)
+            x_sb[q] = xt
             ht = loads.tile([P, 2 * O], BF16, name="h%d" % q)
             nc.sync.dma_start(out=ht[:], in_=h[:, 2 * q : 2 * q + 2, :].rearrange("b u o -> b (u o)"))
-            h_sb.append(ht)
+            h_sb[q] = ht
+            load_input_weights(q, w_in, wn_raw, "wn")
 
-        def load_unit(u, src, lst, nm):
-            t = loads.tile([P, PACK, O], BF16, name="%s%d" % (nm, u))
-            nc.sync.dma_start(out=t[:], in_=src[u].rearrange("(p t) c -> p t c", t=PACK))
-            lst.append(t)
+        def load_hidden(q):
+            for src, store, nm in ((w_hr, whr, "whr"), (w_hz, whz, "whz"), (w_hn, whn, "whn")):
+                t = loads.tile([P, 2, 2 * O], BF16, name="%s%d" % (nm, q))
+                nc.sync.dma_start(out=t[:], in_=src[2 * q : 2 * q + 2].rearrange("u (p e) c -> p u (e c)", e=2))
+                store[q] = t
 
-        def load_bytes(q):
-            t = loads.tile([P, 2, PACK * O], U8, name="wzb%d" % q)
-            nc.sync.dma_start(out=t[:], in_=w_iz_bytes[2 * q : 2 * q + 2].rearrange("u (p t) c -> p u (t c)", t=PACK))
-            wz_bytes.append(t)
-
-        def load_hidden(q, src, lst, nm):
-            t = loads.tile([P, 2, 2 * O], BF16, name="%s%d" % (nm, q))
-            nc.sync.dma_start(out=t[:], in_=src[2 * q : 2 * q + 2].rearrange("u (p e) c -> p u (e c)", e=2))
-            lst.append(t)
-
-        for q in range(PAIRS):
-            load_unit(2 * q, w_ir, wr_raw, "wr")
-            if q == 0:
-                nc.sync.dma_start(out=scl[:], in_=w_iz_scale.rearrange("o (p t) q -> p (o t q)", t=PACK))
-            load_pair_small(q)
-            load_bytes(q)
-            load_unit(2 * q, w_in, wn_raw, "wn")
-            load_hidden(q, w_hr, whr, "whr")
-            load_hidden(q, w_hz, whz, "whz")
-            load_hidden(q, w_hn, whn, "whn")
-            load_unit(2 * q + 1, w_ir, wr_raw, "wr")
-            load_unit(2 * q + 1, w_in, wn_raw, "wn")
+        nc.sync.dma_start(out=scl[:], in_=w_iz_scale.rearrange("o (p t) q -> p (o t q)", t=PACK))
+        load_prep(0)
+        load_prep(1)
+        load_hidden(0)
+        load_prep(2)
+        load_hidden(1)
+        load_prep(3)
+        load_hidden(2)
+        load_hidden(3)
 
         ident_f = const.tile([P, P], F32, name="ident_f")
         make_identity(nc, ident_f[:])
@@ -78,8 +78,8 @@ def tile_unitwisegru_pa_kernel(tc, x, h, w_ir, w_iz_bytes, w_iz_scale, w_in, w_h
         nc.vector.memset(warm_in[:], 0.0)
         nc.scalar.activation(out=warm_out[:], in_=warm_in[:], func=ACT.Sigmoid)
 
-        x_codes, x_scales, h_T = [], [], []
-        codes, scales = {}, {}
+        x_codes, x_scales, h_T = {}, {}, {}
+        rz_codes, rz_scales, n_codes, n_scales = {}, {}, {}, {}
 
         def pair_prep(q):
             words = x_sb[q][:].bitcast(F32)
@@ -106,74 +106,90 @@ def tile_unitwisegru_pa_kernel(tc, x, h, w_ir, w_iz_bytes, w_iz_scale, w_in, w_h
                     )
             hT = loads.tile([P, 4 * P], BF16, name="hT%d" % q)
             nc.scalar.copy(out=hT[:], in_=ht_ps[:])
-            h_T.append(hT)
+            h_T[q] = hT
             xc = loads.tile([P, 2 * P], U32, name="xc%d" % q, align_bytes=64)
             xs = loads.tile([P, 2 * P], U8, name="xs%d" % q, align_bytes=64)
             nc.vector.quantize_mx(out=xc[:].bitcast(FP8X4), scales=xs[:], in_=x_grp[:])
-            x_codes.append(xc)
-            x_scales.append(xs)
+            x_codes[q] = xc
+            x_scales[q] = xs
 
-        def prep(u):
-            q, v = u // 2, u % 2
-            grp = work.tile([P, 3 * PACK * O], BF16, name="grp", tag="grp", align_bytes=64)
-            wz_bf = work.tile([P, PACK, O], BF16, name="wz_bf", tag="wz_bf")
+        def weight_prep(q):
+            wz_bf = work.tile([P, PACK, 2 * O], BF16, name="wz_bf", tag="wz_bf")
             for t in range(PACK):
                 nc.scalar.activation(
                     out=wz_bf[:, t, :],
-                    in_=wz_bytes[q][:, v, t * O : (t + 1) * O].bitcast(FP8),
+                    in_=wz_bytes[q][:, t, :, :].rearrange("p v c -> p (v c)").bitcast(FP8),
                     func=ACT.Copy,
                     scale=scl[:, t : t + 1],
                 )
-
-            def part(g):
-                return grp[:, g * PACK * O : (g + 1) * PACK * O].rearrange("p (c t) -> p c t", t=PACK)
-
-            nc.vector.tensor_copy(out=part(0), in_=wr_raw[u][:].rearrange("p t c -> p c t"))
-            nc.scalar.copy(out=part(1), in_=wz_bf[:].rearrange("p t c -> p c t"))
-            nc.vector.tensor_copy(out=part(2), in_=wn_raw[u][:].rearrange("p t c -> p c t"))
-            cd = work.tile([P, 3 * O], U32, name="cd", tag="cd", align_bytes=64)
-            sc = work.tile([P, 3 * O], U8, name="sc", tag="sc", align_bytes=64)
-            nc.vector.quantize_mx(
-                out=cd[:, 0 : 2 * O].bitcast(FP8X4), scales=sc[:, 0 : 2 * O], in_=grp[:, 0 : 2 * PACK * O]
+            g_rz = work.tile([P, 4 * W], BF16, name="g_rz", tag="g_rz", align_bytes=64)
+            g_n = work.tile([P, 2 * W], BF16, name="g_n", tag="g_n", align_bytes=64)
+            rz_view = g_rz[:].rearrange("p (v g c t) -> p v g c t", v=2, g=2, t=PACK)
+            nc.vector.tensor_copy(
+                out=rz_view[:, :, 0, :, :], in_=wr_raw[q][:].rearrange("p v (t c) -> p v c t", t=PACK)
             )
-            nc.vector.quantize_mx(
-                out=cd[:, 2 * O : 3 * O].bitcast(FP8X4), scales=sc[:, 2 * O : 3 * O], in_=grp[:, 2 * PACK * O : 3 * PACK * O]
+            for v in range(2):
+                src = wz_bf[:, :, v * O : (v + 1) * O].rearrange("p t c -> p c t")
+                if v == 1 and q % 2 == 1:
+                    nc.vector.tensor_copy(out=rz_view[:, v, 1, :, :], in_=src)
+                else:
+                    nc.scalar.copy(out=rz_view[:, v, 1, :, :], in_=src)
+            nc.vector.tensor_copy(
+                out=g_n[:].rearrange("p (v c t) -> p v c t", v=2, t=PACK),
+                in_=wn_raw[q][:].rearrange("p v (t c) -> p v c t", t=PACK),
             )
-            codes[u] = cd
-            scales[u] = sc
+            crz = loads.tile([P, 4 * O], U32, name="crz%d" % q, align_bytes=64)
+            srz = loads.tile([P, 4 * O], U8, name="srz%d" % q, align_bytes=64)
+            nc.vector.quantize_mx(out=crz[:].bitcast(FP8X4), scales=srz[:], in_=g_rz[:])
+            cn = loads.tile([P, 2 * O], U32, name="cn%d" % q, align_bytes=64)
+            sn = loads.tile([P, 2 * O], U8, name="sn%d" % q, align_bytes=64)
+            nc.vector.quantize_mx(out=cn[:].bitcast(FP8X4), scales=sn[:], in_=g_n[:])
+            rz_codes[q], rz_scales[q], n_codes[q], n_scales[q] = crz, srz, cn, sn
 
         def unit(u):
             q, v = u // 2, u % 2
-            rzh_ps = psum.tile([P, 2 * O], F32, name="rzh_ps", tag="rzh")
-            nn_ps = psum.tile([P, 2 * O], F32, name="nn_ps", tag="nn")
-            for dst, wt in ((rzh_ps[:, 0:O], whr), (rzh_ps[:, O : 2 * O], whz), (nn_ps[:, O : 2 * O], whn)):
-                for e in range(2):
-                    nc.tensor.matmul(
-                        out=dst,
-                        lhsT=h_T[q][:, (2 * v + e) * P : (2 * v + e + 1) * P],
-                        rhs=wt[q][:, v, e * O : (e + 1) * O],
-                        start=(e == 0),
-                        stop=(e == 1),
-                    )
-            hs = epi.tile([P, 2 * O], F32, name="hs", tag="hs")
-            nc.scalar.copy(out=hs[:], in_=rzh_ps[:])
-            rzx_ps = psum.tile([P, 2 * O], F32, name="rzx_ps", tag="rzx")
             xl = x_codes[q][:, v * P : (v + 1) * P].bitcast(FP8X4)
             xls = x_scales[q][:, v * P : (v + 1) * P]
-            nc.tensor.matmul_mx(
-                out=rzx_ps[:], lhsT=xl, lhsT_scale=xls,
-                rhs=codes[u][:, 0 : 2 * O].bitcast(FP8X4), rhs_scale=scales[u][:, 0 : 2 * O],
-                start=True, stop=True,
-            )
+            rzT_ps = psum.tile([P, 4 * P], F32, name="rzT_ps", tag="rzT")
+            for k in range(4):
+                wcols = slice(v * 2 * O + k * P, v * 2 * O + (k + 1) * P)
+                nc.tensor.matmul_mx(
+                    out=rzT_ps[:, k * P : (k + 1) * P],
+                    lhsT=rz_codes[q][:, wcols].bitcast(FP8X4), lhsT_scale=rz_scales[q][:, wcols],
+                    rhs=xl, rhs_scale=xls, start=True, stop=True,
+                )
+            rzT = epi.tile([P, 4 * P], F32, name="rzT", tag="rzT_sb")
+            nc.scalar.copy(out=rzT[:], in_=rzT_ps[:])
+            nn_ps = psum.tile([P, 2 * O], F32, name="nn_ps", tag="nn")
+            for e in range(2):
+                nc.tensor.matmul(
+                    out=nn_ps[:, O : 2 * O],
+                    lhsT=h_T[q][:, (2 * v + e) * P : (2 * v + e + 1) * P],
+                    rhs=whn[q][:, v, e * O : (e + 1) * O],
+                    start=(e == 0), stop=(e == 1),
+                )
             nc.tensor.matmul_mx(
                 out=nn_ps[:, 0:O], lhsT=xl, lhsT_scale=xls,
-                rhs=codes[u][:, 2 * O : 3 * O].bitcast(FP8X4), rhs_scale=scales[u][:, 2 * O : 3 * O],
+                rhs=n_codes[q][:, v * O : (v + 1) * O].bitcast(FP8X4), rhs_scale=n_scales[q][:, v * O : (v + 1) * O],
                 start=True, stop=True,
             )
-            pre = epi.tile([P, 2 * O], F32, name="pre", tag="pre")
-            nc.vector.tensor_tensor(out=pre[:], in0=rzx_ps[:], in1=hs[:], op=ALU.add)
+            rz_ps = psum.tile([P, 2 * O], F32, name="rz_ps", tag="rzh")
+            for g, wt in ((0, whr), (1, whz)):
+                for e in range(2):
+                    nc.tensor.matmul(
+                        out=rz_ps[:, g * O : (g + 1) * O],
+                        lhsT=h_T[q][:, (2 * v + e) * P : (2 * v + e + 1) * P],
+                        rhs=wt[q][:, v, e * O : (e + 1) * O],
+                        start=(e == 0), stop=False,
+                    )
+                for k in (2 * g, 2 * g + 1):
+                    cols = slice(k * P, (k + 1) * P)
+                    nc.tensor.matmul(
+                        out=rz_ps[:, cols], lhsT=rzT[:, cols], rhs=ident_f[:],
+                        is_transpose=True, start=False, stop=(k == 2 * g + 1),
+                    )
             rz = epi.tile([P, 2 * O], F32, name="rz", tag="rz")
-            nc.scalar.activation(out=rz[:], in_=pre[:], func=ACT.Sigmoid)
+            nc.scalar.activation(out=rz[:], in_=rz_ps[:], func=ACT.Sigmoid)
             rh = epi.tile([P, O], F32, name="rh", tag="rh")
             nc.vector.tensor_tensor(out=rh[:], in0=nn_ps[:, O : 2 * O], in1=rz[:, 0:O], op=ALU.mult)
             npre = epi.tile([P, O], F32, name="npre", tag="npre")
@@ -190,13 +206,8 @@ def tile_unitwisegru_pa_kernel(tc, x, h, w_ir, w_iz_bytes, w_iz_scale, w_in, w_h
             nc.vector.tensor_tensor(out=res[:], in0=zp[:], in1=zn[:], op=ALU.subtract)
             nc.sync.dma_start(out=out[:, u, :], in_=res[:])
 
-        pair_prep(0)
-        for u in range(AHEAD):
-            prep(u)
+        for q in range(PAIRS):
+            pair_prep(q)
+            weight_prep(q)
         for u in range(U):
-            nxt = u + AHEAD
-            if nxt < U and nxt % 2 == 0:
-                pair_prep(nxt // 2)
             unit(u)
-            if nxt < U:
-                prep(nxt)

@@ -26,32 +26,31 @@ def tile_unitwisegru_pa_kernel(tc, x, h, w_ir, w_iz_bytes, w_iz_scale, w_in, w_h
     with ExitStack() as ctx:
         const = ctx.enter_context(tc.tile_pool(name="const", bufs=1))
         loads = ctx.enter_context(tc.tile_pool(name="loads", bufs=1))
-        work = ctx.enter_context(tc.tile_pool(name="work", bufs=2))
-        epi = ctx.enter_context(tc.tile_pool(name="epi", bufs=3))
+        work = ctx.enter_context(tc.tile_pool(name="work", bufs=3))
+        epi = ctx.enter_context(tc.tile_pool(name="epi", bufs=4))
         psum = ctx.enter_context(tc.psum_pool(name="psum", bufs=2))
 
         x_sb, h_sb, wr_raw, wn_raw, wz_bytes, whr, whz, whn = {}, {}, {}, {}, {}, {}, {}, {}
         scl = const.tile([P, PACK], F32, name="scl")
 
-        def load_input_weights(q, src, store, nm):
-            t = loads.tile([P, 2, W], BF16, name="%s%d" % (nm, q))
-            for v in range(2):
-                nc.sync.dma_start(out=t[:, v, :], in_=src[2 * q + v].rearrange("(p t) c -> p (t c)", t=PACK))
-            store[q] = t
-
         def load_prep(q):
             zb = loads.tile([P, PACK, 2, O], U8, name="wzb%d" % q)
+            wr = loads.tile([P, 2, W], BF16, name="wr%d" % q)
+            wn = loads.tile([P, 2, W], BF16, name="wn%d" % q)
+            wz_bytes[q], wr_raw[q], wn_raw[q] = zb, wr, wn
             for v in range(2):
+                nc.sync.dma_start(out=wr[:, v, :], in_=w_ir[2 * q + v].rearrange("(p t) c -> p (t c)", t=PACK))
                 nc.sync.dma_start(out=zb[:, :, v, :], in_=w_iz_bytes[2 * q + v].rearrange("(p t) c -> p t c", t=PACK))
-            wz_bytes[q] = zb
-            load_input_weights(q, w_ir, wr_raw, "wr")
+                if q == 0 and v == 0:
+                    nc.sync.dma_start(out=scl[:], in_=w_iz_scale.rearrange("o (p t) q -> p (o t q)", t=PACK))
+            for v in range(2):
+                nc.sync.dma_start(out=wn[:, v, :], in_=w_in[2 * q + v].rearrange("(p t) c -> p (t c)", t=PACK))
             xt = loads.tile([P, 2 * I], BF16, name="x%d" % q)
             nc.sync.dma_start(out=xt[:], in_=x[:, 2 * q : 2 * q + 2, :].rearrange("b u i -> b (u i)"))
             x_sb[q] = xt
             ht = loads.tile([P, 2 * O], BF16, name="h%d" % q)
             nc.sync.dma_start(out=ht[:], in_=h[:, 2 * q : 2 * q + 2, :].rearrange("b u o -> b (u o)"))
             h_sb[q] = ht
-            load_input_weights(q, w_in, wn_raw, "wn")
 
         def load_hidden(q):
             for src, store, nm in ((w_hr, whr, "whr"), (w_hz, whz, "whz"), (w_hn, whn, "whn")):
@@ -59,7 +58,6 @@ def tile_unitwisegru_pa_kernel(tc, x, h, w_ir, w_iz_bytes, w_iz_scale, w_in, w_h
                 nc.sync.dma_start(out=t[:], in_=src[2 * q : 2 * q + 2].rearrange("u (p e) c -> p u (e c)", e=2))
                 store[q] = t
 
-        nc.sync.dma_start(out=scl[:], in_=w_iz_scale.rearrange("o (p t) q -> p (o t q)", t=PACK))
         load_prep(0)
         load_prep(1)
         load_hidden(0)
@@ -80,10 +78,11 @@ def tile_unitwisegru_pa_kernel(tc, x, h, w_ir, w_iz_bytes, w_iz_scale, w_in, w_h
 
         x_codes, x_scales, h_T = {}, {}, {}
         rz_codes, rz_scales, n_codes, n_scales = {}, {}, {}, {}
+        grouped = {}
 
         def pair_prep(q):
             words = x_sb[q][:].bitcast(F32)
-            xt_ps = psum.tile([P, 4 * P], F32, name="xt_ps", tag="tp")
+            xt_ps = psum.tile([P, 4 * P], F32, name="xt_ps", tag="bankA")
             for v in range(2):
                 for s in range(2):
                     nc.tensor.transpose(
@@ -96,7 +95,7 @@ def tile_unitwisegru_pa_kernel(tc, x, h, w_ir, w_iz_bytes, w_iz_scale, w_in, w_h
                 out=x_grp[:].bitcast(F32).rearrange("p (v r s) -> p v r s", v=2, s=2),
                 in_=xt_ps[:].rearrange("p (v s r) -> p v r s", v=2, s=2),
             )
-            ht_ps = psum.tile([P, 4 * P], BF16, name="ht_ps", tag="tp")
+            ht_ps = psum.tile([P, 4 * P], BF16, name="ht_ps", tag="bankA")
             for v in range(2):
                 for e in range(2):
                     nc.tensor.transpose(
@@ -114,30 +113,41 @@ def tile_unitwisegru_pa_kernel(tc, x, h, w_ir, w_iz_bytes, w_iz_scale, w_in, w_h
             x_scales[q] = xs
 
         def weight_prep(q):
+            groups = ((0, 1), (1, 2)) if q == 0 else ((0, 2),)
             wz_bf = work.tile([P, PACK, 2 * O], BF16, name="wz_bf", tag="wz_bf")
-            for t in range(PACK):
-                nc.scalar.activation(
-                    out=wz_bf[:, t, :],
-                    in_=wz_bytes[q][:, t, :, :].rearrange("p v c -> p (v c)").bitcast(FP8),
-                    func=ACT.Copy,
-                    scale=scl[:, t : t + 1],
-                )
             g_rz = work.tile([P, 4 * W], BF16, name="g_rz", tag="g_rz", align_bytes=64)
             g_n = work.tile([P, 2 * W], BF16, name="g_n", tag="g_n", align_bytes=64)
             rz_view = g_rz[:].rearrange("p (v g c t) -> p v g c t", v=2, g=2, t=PACK)
-            nc.vector.tensor_copy(
-                out=rz_view[:, :, 0, :, :], in_=wr_raw[q][:].rearrange("p v (t c) -> p v c t", t=PACK)
-            )
+            n_view = g_n[:].rearrange("p (v c t) -> p v c t", v=2, t=PACK)
+            for v0, v1 in groups:
+                for t in range(PACK):
+                    nc.scalar.activation(
+                        out=wz_bf[:, t, v0 * O : v1 * O],
+                        in_=wz_bytes[q][:, t, v0:v1, :].rearrange("p v c -> p (v c)").bitcast(FP8),
+                        func=ACT.Copy,
+                        scale=scl[:, t : t + 1],
+                    )
             for v in range(2):
-                src = wz_bf[:, :, v * O : (v + 1) * O].rearrange("p t c -> p c t")
-                if v == 1 and q % 2 == 1:
-                    nc.vector.tensor_copy(out=rz_view[:, v, 1, :, :], in_=src)
+                nc.vector.tensor_copy(
+                    out=rz_view[:, v, 0, :, :].rearrange("p (c i) t -> p c t i", i=4),
+                    in_=wr_raw[q][:, v, :].rearrange("p (t c i) -> p c t i", t=PACK, i=4),
+                )
+            for v in range(2):
+                nc.vector.tensor_copy(
+                    out=n_view[:, v, :, :].rearrange("p (c i) t -> p c t i", i=4),
+                    in_=wn_raw[q][:, v, :].rearrange("p (t c i) -> p c t i", t=PACK, i=4),
+                )
+            for v in range(2):
+                src = wz_bf[:, :, v * O : (v + 1) * O].rearrange("p t (c i) -> p c t i", i=4)
+                dst = rz_view[:, v, 1, :, :].rearrange("p (c i) t -> p c t i", i=4)
+                if v == 1 and q >= 1:
+                    nc.vector.tensor_copy(out=dst, in_=src)
                 else:
-                    nc.scalar.copy(out=rz_view[:, v, 1, :, :], in_=src)
-            nc.vector.tensor_copy(
-                out=g_n[:].rearrange("p (v c t) -> p v c t", v=2, t=PACK),
-                in_=wn_raw[q][:].rearrange("p v (t c) -> p v c t", t=PACK),
-            )
+                    nc.scalar.copy(out=dst, in_=src)
+            grouped[q] = (g_rz, g_n)
+
+        def weight_quantize(q):
+            g_rz, g_n = grouped[q]
             crz = loads.tile([P, 4 * O], U32, name="crz%d" % q, align_bytes=64)
             srz = loads.tile([P, 4 * O], U8, name="srz%d" % q, align_bytes=64)
             nc.vector.quantize_mx(out=crz[:].bitcast(FP8X4), scales=srz[:], in_=g_rz[:])
@@ -150,7 +160,7 @@ def tile_unitwisegru_pa_kernel(tc, x, h, w_ir, w_iz_bytes, w_iz_scale, w_in, w_h
             q, v = u // 2, u % 2
             xl = x_codes[q][:, v * P : (v + 1) * P].bitcast(FP8X4)
             xls = x_scales[q][:, v * P : (v + 1) * P]
-            rzT_ps = psum.tile([P, 4 * P], F32, name="rzT_ps", tag="rzT")
+            rzT_ps = psum.tile([P, 4 * P], F32, name="rzT_ps", tag="bankA")
             for k in range(4):
                 wcols = slice(v * 2 * O + k * P, v * 2 * O + (k + 1) * P)
                 nc.tensor.matmul_mx(
@@ -160,7 +170,7 @@ def tile_unitwisegru_pa_kernel(tc, x, h, w_ir, w_iz_bytes, w_iz_scale, w_in, w_h
                 )
             rzT = epi.tile([P, 4 * P], F32, name="rzT", tag="rzT_sb")
             nc.scalar.copy(out=rzT[:], in_=rzT_ps[:])
-            nn_ps = psum.tile([P, 2 * O], F32, name="nn_ps", tag="nn")
+            nn_ps = psum.tile([P, 2 * O], F32, name="nn_ps", tag="nn", bufs=3)
             for e in range(2):
                 nc.tensor.matmul(
                     out=nn_ps[:, O : 2 * O],
@@ -173,7 +183,7 @@ def tile_unitwisegru_pa_kernel(tc, x, h, w_ir, w_iz_bytes, w_iz_scale, w_in, w_h
                 rhs=n_codes[q][:, v * O : (v + 1) * O].bitcast(FP8X4), rhs_scale=n_scales[q][:, v * O : (v + 1) * O],
                 start=True, stop=True,
             )
-            rz_ps = psum.tile([P, 2 * O], F32, name="rz_ps", tag="rzh")
+            rz_ps = psum.tile([P, 2 * O], F32, name="rz_ps", tag="rzh", bufs=3)
             for g, wt in ((0, whr), (1, whz)):
                 for e in range(2):
                     nc.tensor.matmul(
@@ -206,8 +216,15 @@ def tile_unitwisegru_pa_kernel(tc, x, h, w_ir, w_iz_bytes, w_iz_scale, w_in, w_h
             nc.vector.tensor_tensor(out=res[:], in0=zp[:], in1=zn[:], op=ALU.subtract)
             nc.sync.dma_start(out=out[:, u, :], in_=res[:])
 
-        for q in range(PAIRS):
-            pair_prep(q)
+        def prep(q):
             weight_prep(q)
-        for u in range(U):
-            unit(u)
+            pair_prep(q)
+            weight_quantize(q)
+
+        prep(0)
+        prep(1)
+        for q in range(PAIRS):
+            unit(2 * q)
+            unit(2 * q + 1)
+            if q + 2 < PAIRS:
+                prep(q + 2)

@@ -34,15 +34,16 @@ def tile_unitwisegru_pa_kernel(tc, x, h, w_ir, w_iz_bytes, w_iz_scale, w_in, w_h
         scl = const.tile([P, PACK], F32, name="scl")
 
         def load_prep(q):
-            zb = loads.tile([P, PACK, 2, O], U8, name="wzb%d" % q)
+            zb = loads.tile([P, 2, PACK, O] if q == 0 else [P, PACK, 2, O], U8, name="wzb%d" % q)
             wr = loads.tile([P, 2, W], BF16, name="wr%d" % q)
             wn = loads.tile([P, 2, W], BF16, name="wn%d" % q)
             wz_bytes[q], wr_raw[q], wn_raw[q] = zb, wr, wn
             for v in range(2):
                 nc.sync.dma_start(out=wr[:, v, :], in_=w_ir[2 * q + v].rearrange("(p t) c -> p (t c)", t=PACK))
-                nc.sync.dma_start(out=zb[:, :, v, :], in_=w_iz_bytes[2 * q + v].rearrange("(p t) c -> p t c", t=PACK))
-                if q == 0 and v == 0:
-                    nc.sync.dma_start(out=scl[:], in_=w_iz_scale.rearrange("o (p t) q -> p (o t q)", t=PACK))
+                nc.sync.dma_start(
+                    out=zb[:, v, :, :] if q == 0 else zb[:, :, v, :],
+                    in_=w_iz_bytes[2 * q + v].rearrange("(p t) c -> p t c", t=PACK),
+                )
             for v in range(2):
                 nc.sync.dma_start(out=wn[:, v, :], in_=w_in[2 * q + v].rearrange("(p t) c -> p (t c)", t=PACK))
             xt = loads.tile([P, 2 * I], BF16, name="x%d" % q)
@@ -58,6 +59,7 @@ def tile_unitwisegru_pa_kernel(tc, x, h, w_ir, w_iz_bytes, w_iz_scale, w_in, w_h
                 nc.sync.dma_start(out=t[:], in_=src[2 * q : 2 * q + 2].rearrange("u (p e) c -> p u (e c)", e=2))
                 store[q] = t
 
+        nc.scalar.dma_start(out=scl[:], in_=w_iz_scale.rearrange("o (p t) q -> p (o t q)", t=PACK))
         load_prep(0)
         load_prep(1)
         load_hidden(0)
@@ -79,6 +81,7 @@ def tile_unitwisegru_pa_kernel(tc, x, h, w_ir, w_iz_bytes, w_iz_scale, w_in, w_h
         x_codes, x_scales, h_T = {}, {}, {}
         rz_codes, rz_scales, n_codes, n_scales = {}, {}, {}, {}
         grouped = {}
+        pending = {}
 
         def pair_prep(q):
             words = x_sb[q][:].bitcast(F32)
@@ -123,7 +126,9 @@ def tile_unitwisegru_pa_kernel(tc, x, h, w_ir, w_iz_bytes, w_iz_scale, w_in, w_h
                 for t in range(PACK):
                     nc.scalar.activation(
                         out=wz_bf[:, t, v0 * O : v1 * O],
-                        in_=wz_bytes[q][:, t, v0:v1, :].rearrange("p v c -> p (v c)").bitcast(FP8),
+                        in_=(
+                            wz_bytes[q][:, v0, t, :] if q == 0 else wz_bytes[q][:, t, :, :].rearrange("p v c -> p (v c)")
+                        ).bitcast(FP8),
                         func=ACT.Copy,
                         scale=scl[:, t : t + 1],
                     )
@@ -202,19 +207,31 @@ def tile_unitwisegru_pa_kernel(tc, x, h, w_ir, w_iz_bytes, w_iz_scale, w_in, w_h
             nc.scalar.activation(out=rz[:], in_=rz_ps[:], func=ACT.Sigmoid)
             rh = epi.tile([P, O], F32, name="rh", tag="rh")
             nc.vector.tensor_tensor(out=rh[:], in0=nn_ps[:, O : 2 * O], in1=rz[:, 0:O], op=ALU.mult)
-            npre = epi.tile([P, O], F32, name="npre", tag="npre")
-            nc.vector.tensor_tensor(out=npre[:], in0=nn_ps[:, 0:O], in1=rh[:], op=ALU.add)
+            blend_first(u - 1)
             zp = epi.tile([P, O], F32, name="zp", tag="zp")
             nc.vector.tensor_tensor(out=zp[:], in0=rz[:, O : 2 * O], in1=h_sb[q][:, v * O : (v + 1) * O], op=ALU.mult)
+            blend_second(u - 1)
+            npre = epi.tile([P, O], F32, name="npre", tag="npre")
+            nc.vector.tensor_tensor(out=npre[:], in0=nn_ps[:, 0:O], in1=rh[:], op=ALU.add)
             nt = epi.tile([P, O], F32, name="nt", tag="nt")
             nc.scalar.activation(out=nt[:], in_=npre[:], func=ACT.Tanh)
-            zn = epi.tile([P, O], F32, name="zn", tag="zn")
-            nc.vector.scalar_tensor_tensor(
-                out=zn[:], in0=rz[:, O : 2 * O], scalar=1.0, in1=nt[:], op0=ALU.subtract, op1=ALU.mult
-            )
-            res = epi.tile([P, O], F32, name="res", tag="res")
-            nc.vector.tensor_tensor(out=res[:], in0=zp[:], in1=zn[:], op=ALU.subtract)
-            nc.sync.dma_start(out=out[:, u, :], in_=res[:])
+            pending[u] = (rz, zp, nt)
+
+        def blend_first(u):
+            if u >= 0:
+                rz, zp, nt = pending[u]
+                zn = epi.tile([P, O], F32, name="zn", tag="zn")
+                nc.vector.scalar_tensor_tensor(
+                    out=zn[:], in0=rz[:, O : 2 * O], scalar=1.0, in1=nt[:], op0=ALU.subtract, op1=ALU.mult
+                )
+                pending[u] = (zp, zn)
+
+        def blend_second(u):
+            if u >= 0:
+                zp, zn = pending[u]
+                res = epi.tile([P, O], F32, name="res", tag="res")
+                nc.vector.tensor_tensor(out=res[:], in0=zp[:], in1=zn[:], op=ALU.subtract)
+                nc.sync.dma_start(out=out[:, u, :], in_=res[:])
 
         def prep(q):
             weight_prep(q)
@@ -228,3 +245,5 @@ def tile_unitwisegru_pa_kernel(tc, x, h, w_ir, w_iz_bytes, w_iz_scale, w_in, w_h
             unit(2 * q + 1)
             if q + 2 < PAIRS:
                 prep(q + 2)
+        blend_first(U - 1)
+        blend_second(U - 1)

@@ -34,9 +34,9 @@ def tile_unitwisegru_pa_kernel(tc, x, h, w_ir, w_iz_bytes, w_iz_scale, w_in, w_h
         scl = const.tile([P, PACK], F32, name="scl")
 
         def load_prep(q):
-            zb = loads.tile([P, 2, PACK, O] if q == 0 else [P, PACK, 2, O], U8, name="wzb%d" % q)
-            wr = loads.tile([P, 2, W], BF16, name="wr%d" % q)
-            wn = loads.tile([P, 2, W], BF16, name="wn%d" % q)
+            zb = loads.tile([P, 2, PACK, O] if q == 0 else [P, PACK, 2, O], U8, name="wzb%d" % q, align_bytes=256)
+            wr = loads.tile([P, 2, W], BF16, name="wr%d" % q, align_bytes=256)
+            wn = loads.tile([P, 2, W], BF16, name="wn%d" % q, align_bytes=256)
             wz_bytes[q], wr_raw[q], wn_raw[q] = zb, wr, wn
             for v in range(2):
                 nc.sync.dma_start(out=wr[:, v, :], in_=w_ir[2 * q + v].rearrange("(p t) c -> p (t c)", t=PACK))
@@ -46,16 +46,16 @@ def tile_unitwisegru_pa_kernel(tc, x, h, w_ir, w_iz_bytes, w_iz_scale, w_in, w_h
                 )
             for v in range(2):
                 nc.sync.dma_start(out=wn[:, v, :], in_=w_in[2 * q + v].rearrange("(p t) c -> p (t c)", t=PACK))
-            xt = loads.tile([P, 2 * I], BF16, name="x%d" % q)
+            xt = loads.tile([P, 2 * I], BF16, name="x%d" % q, align_bytes=256)
             nc.sync.dma_start(out=xt[:], in_=x[:, 2 * q : 2 * q + 2, :].rearrange("b u i -> b (u i)"))
             x_sb[q] = xt
-            ht = loads.tile([P, 2 * O], BF16, name="h%d" % q)
+            ht = loads.tile([P, 2 * O], BF16, name="h%d" % q, align_bytes=256)
             nc.sync.dma_start(out=ht[:], in_=h[:, 2 * q : 2 * q + 2, :].rearrange("b u o -> b (u o)"))
             h_sb[q] = ht
 
         def load_hidden(q):
             for src, store, nm in ((w_hr, whr, "whr"), (w_hz, whz, "whz"), (w_hn, whn, "whn")):
-                t = loads.tile([P, 2, 2 * O], BF16, name="%s%d" % (nm, q))
+                t = loads.tile([P, 2, 2 * O], BF16, name="%s%d" % (nm, q), align_bytes=256)
                 nc.sync.dma_start(out=t[:], in_=src[2 * q : 2 * q + 2].rearrange("u (p e) c -> p u (e c)", e=2))
                 store[q] = t
 
@@ -229,7 +229,7 @@ def tile_unitwisegru_pa_kernel(tc, x, h, w_ir, w_iz_bytes, w_iz_scale, w_in, w_h
         def blend_second(u):
             if u >= 0:
                 zp, zn = pending[u]
-                res = epi.tile([P, O], F32, name="res", tag="res")
+                res = epi.tile([P, O], F32, name="res", tag="res", align_bytes=256)
                 nc.vector.tensor_tensor(out=res[:], in0=zp[:], in1=zn[:], op=ALU.subtract)
                 nc.sync.dma_start(out=out[:, u, :], in_=res[:])
 

from contextlib import ExitStack

import concourse.mybir as mybir
from concourse.masks import make_identity

B, U, I, O = 128, 8, 512, 256
FLOPS = 2 * B * U * O * 3 * (I + O)

F32 = mybir.dt.float32
BF16 = mybir.dt.bfloat16
U32 = mybir.dt.uint32
U8 = mybir.dt.uint8
FP8 = mybir.dt.float8_e4m3fn
FP8X4 = mybir.dt.float8_e4m3fn_x4
ACT = mybir.ActivationFunctionType
ALU = mybir.AluOpType

P = 128
PACK = 4
PAIRS = U // 2
W = PACK * O


def tile_unitwisegru_pa_kernel(tc, x, h, w_ir, w_iz_bytes, w_iz_scale, w_in, w_hr, w_hz, w_hn, out):
    nc = tc.nc
    with ExitStack() as ctx:
        const = ctx.enter_context(tc.tile_pool(name="const", bufs=1))
        loads = ctx.enter_context(tc.tile_pool(name="loads", bufs=1))
        work = ctx.enter_context(tc.tile_pool(name="work", bufs=3))
        epi = ctx.enter_context(tc.tile_pool(name="epi", bufs=4))
        psum = ctx.enter_context(tc.psum_pool(name="psum", bufs=2))

        x_sb, h_sb, wr_raw, wn_raw, wz_bytes, whr, whz, whn = {}, {}, {}, {}, {}, {}, {}, {}
        scl = const.tile([P, PACK], F32, name="scl")

        def load_prep(q):
            zb = loads.tile([P, 2, PACK, O] if q == 0 else [P, PACK, 2, O], U8, name="wzb%d" % q, align_bytes=256)
            wr = loads.tile([P, 2, W], BF16, name="wr%d" % q, align_bytes=256)
            wn = loads.tile([P, 2, W], BF16, name="wn%d" % q, align_bytes=256)
            wz_bytes[q], wr_raw[q], wn_raw[q] = zb, wr, wn
            for v in range(2):
                nc.sync.dma_start(out=wr[:, v, :], in_=w_ir[2 * q + v].rearrange("(p t) c -> p (t c)", t=PACK))
                nc.sync.dma_start(
                    out=zb[:, v, :, :] if q == 0 else zb[:, :, v, :],
                    in_=w_iz_bytes[2 * q + v].rearrange("(p t) c -> p t c", t=PACK),
                )
            for v in range(2):
                nc.sync.dma_start(out=wn[:, v, :], in_=w_in[2 * q + v].rearrange("(p t) c -> p (t c)", t=PACK))
            xt = loads.tile([P, 2 * I], BF16, name="x%d" % q, align_bytes=256)
            nc.sync.dma_start(out=xt[:], in_=x[:, 2 * q : 2 * q + 2, :].rearrange("b u i -> b (u i)"))
            x_sb[q] = xt
            ht = loads.tile([P, 2 * O], BF16, name="h%d" % q, align_bytes=256)
            nc.sync.dma_start(out=ht[:], in_=h[:, 2 * q : 2 * q + 2, :].rearrange("b u o -> b (u o)"))
            h_sb[q] = ht

        def load_hidden(q):
            for src, store, nm in ((w_hr, whr, "whr"), (w_hz, whz, "whz"), (w_hn, whn, "whn")):
                t = loads.tile([P, 2, 2 * O], BF16, name="%s%d" % (nm, q), align_bytes=256)
                nc.sync.dma_start(out=t[:], in_=src[2 * q : 2 * q + 2].rearrange("u (p e) c -> p u (e c)", e=2))
                store[q] = t

        nc.scalar.dma_start(out=scl[:], in_=w_iz_scale.rearrange("o (p t) q -> p (o t q)", t=PACK))
        load_prep(0)
        load_prep(1)
        load_hidden(0)
        load_prep(2)
        load_hidden(1)
        load_prep(3)
        load_hidden(2)
        load_hidden(3)

        ident_f = const.tile([P, P], F32, name="ident_f")
        make_identity(nc, ident_f[:])
        ident_b = const.tile([P, P], BF16, name="ident_b")
        make_identity(nc, ident_b[:])
        warm_in = const.tile([P, 1], F32, name="warm_in")
        warm_out = const.tile([P, 1], F32, name="warm_out")
        nc.vector.memset(warm_in[:], 0.0)
        nc.scalar.activation(out=warm_out[:], in_=warm_in[:], func=ACT.Sigmoid)

        x_codes, x_scales, h_T = {}, {}, {}
        rz_codes, rz_scales, n_codes, n_scales = {}, {}, {}, {}
        grouped = {}
        pending = {}

        def pair_prep(q):
            words = x_sb[q][:].bitcast(F32)
            xt_ps = psum.tile([P, 4 * P], F32, name="xt_ps", tag="bankA")
            for v in range(2):
                for s in range(2):
                    nc.tensor.transpose(
                        xt_ps[:, (2 * v + s) * P : (2 * v + s + 1) * P],
                        words[:, 256 * v + s : 256 * (v + 1) : 2],
                        ident_f[:],
                    )
            x_grp = work.tile([P, 2 * P * PACK], BF16, name="x_grp", tag="x_grp", align_bytes=64)
            nc.scalar.copy(
                out=x_grp[:].bitcast(F32).rearrange("p (v r s) -> p v r s", v=2, s=2),
                in_=xt_ps[:].rearrange("p (v s r) -> p v r s", v=2, s=2),
            )
            ht_ps = psum.tile([P, 4 * P], BF16, name="ht_ps", tag="bankA")
            for v in range(2):
                for e in range(2):
                    nc.tensor.transpose(
                        ht_ps[:, (2 * v + e) * P : (2 * v + e + 1) * P],
                        h_sb[q][:, O * v + e : O * (v + 1) : 2],
                        ident_b[:],
                    )
            hT = loads.tile([P, 4 * P], BF16, name="hT%d" % q)
            nc.scalar.copy(out=hT[:], in_=ht_ps[:])
            h_T[q] = hT
            xc = loads.tile([P, 2 * P], U32, name="xc%d" % q, align_bytes=64)
            xs = loads.tile([P, 2 * P], U8, name="xs%d" % q, align_bytes=64)
            nc.vector.quantize_mx(out=xc[:].bitcast(FP8X4), scales=xs[:], in_=x_grp[:])
            x_codes[q] = xc
            x_scales[q] = xs

        def weight_prep(q):
            groups = ((0, 1), (1, 2)) if q == 0 else ((0, 2),)
            wz_bf = work.tile([P, PACK, 2 * O], BF16, name="wz_bf", tag="wz_bf")
            g_rz = work.tile([P, 4 * W], BF16, name="g_rz", tag="g_rz", align_bytes=64)
            g_n = work.tile([P, 2 * W], BF16, name="g_n", tag="g_n", align_bytes=64)
            rz_view = g_rz[:].rearrange("p (v g c t) -> p v g c t", v=2, g=2, t=PACK)
            n_view = g_n[:].rearrange("p (v c t) -> p v c t", v=2, t=PACK)
            for v0, v1 in groups:
                for t in range(PACK):
                    nc.scalar.activation(
                        out=wz_bf[:, t, v0 * O : v1 * O],
                        in_=(
                            wz_bytes[q][:, v0, t, :] if q == 0 else wz_bytes[q][:, t, :, :].rearrange("p v c -> p (v c)")
                        ).bitcast(FP8),
                        func=ACT.Copy,
                        scale=scl[:, t : t + 1],
                    )
            for v in range(2):
                nc.vector.tensor_copy(
                    out=rz_view[:, v, 0, :, :].rearrange("p (c i) t -> p c t i", i=4),
                    in_=wr_raw[q][:, v, :].rearrange("p (t c i) -> p c t i", t=PACK, i=4),
                )
            for v in range(2):
                nc.vector.tensor_copy(
                    out=n_view[:, v, :, :].rearrange("p (c i) t -> p c t i", i=4),
                    in_=wn_raw[q][:, v, :].rearrange("p (t c i) -> p c t i", t=PACK, i=4),
                )
            for v in range(2):
                src = wz_bf[:, :, v * O : (v + 1) * O].rearrange("p t (c i) -> p c t i", i=4)
                dst = rz_view[:, v, 1, :, :].rearrange("p (c i) t -> p c t i", i=4)
                if v == 1 and q >= 1:
                    nc.vector.tensor_copy(out=dst, in_=src)
                else:
                    nc.scalar.copy(out=dst, in_=src)
            grouped[q] = (g_rz, g_n)

        def weight_quantize(q):
            g_rz, g_n = grouped[q]
            crz = loads.tile([P, 4 * O], U32, name="crz%d" % q, align_bytes=64)
            srz = loads.tile([P, 4 * O], U8, name="srz%d" % q, align_bytes=64)
            nc.vector.quantize_mx(out=crz[:].bitcast(FP8X4), scales=srz[:], in_=g_rz[:])
            cn = loads.tile([P, 2 * O], U32, name="cn%d" % q, align_bytes=64)
            sn = loads.tile([P, 2 * O], U8, name="sn%d" % q, align_bytes=64)
            nc.vector.quantize_mx(out=cn[:].bitcast(FP8X4), scales=sn[:], in_=g_n[:])
            rz_codes[q], rz_scales[q], n_codes[q], n_scales[q] = crz, srz, cn, sn

        def unit(u):
            q, v = u // 2, u % 2
            xl = x_codes[q][:, v * P : (v + 1) * P].bitcast(FP8X4)
            xls = x_scales[q][:, v * P : (v + 1) * P]
            rzT_ps = psum.tile([P, 4 * P], F32, name="rzT_ps", tag="bankA")
            for k in range(4):
                wcols = slice(v * 2 * O + k * P, v * 2 * O + (k + 1) * P)
                nc.tensor.matmul_mx(
                    out=rzT_ps[:, k * P : (k + 1) * P],
                    lhsT=rz_codes[q][:, wcols].bitcast(FP8X4), lhsT_scale=rz_scales[q][:, wcols],
                    rhs=xl, rhs_scale=xls, start=True, stop=True,
                )
            rzT = epi.tile([P, 4 * P], F32, name="rzT", tag="rzT_sb")
            nc.scalar.copy(out=rzT[:], in_=rzT_ps[:])
            nn_ps = psum.tile([P, 2 * O], F32, name="nn_ps", tag="nn", bufs=3)
            for e in range(2):
                nc.tensor.matmul(
                    out=nn_ps[:, O : 2 * O],
                    lhsT=h_T[q][:, (2 * v + e) * P : (2 * v + e + 1) * P],
                    rhs=whn[q][:, v, e * O : (e + 1) * O],
                    start=(e == 0), stop=(e == 1),
                )
            nc.tensor.matmul_mx(
                out=nn_ps[:, 0:O], lhsT=xl, lhsT_scale=xls,
                rhs=n_codes[q][:, v * O : (v + 1) * O].bitcast(FP8X4), rhs_scale=n_scales[q][:, v * O : (v + 1) * O],
                start=True, stop=True,
            )
            rz_ps = psum.tile([P, 2 * O], F32, name="rz_ps", tag="rzh", bufs=3)
            for g, wt in ((0, whr), (1, whz)):
                for e in range(2):
                    nc.tensor.matmul(
                        out=rz_ps[:, g * O : (g + 1) * O],
                        lhsT=h_T[q][:, (2 * v + e) * P : (2 * v + e + 1) * P],
                        rhs=wt[q][:, v, e * O : (e + 1) * O],
                        start=(e == 0), stop=False,
                    )
                for k in (2 * g, 2 * g + 1):
                    cols = slice(k * P, (k + 1) * P)
                    nc.tensor.matmul(
                        out=rz_ps[:, cols], lhsT=rzT[:, cols], rhs=ident_f[:],
                        is_transpose=True, start=False, stop=(k == 2 * g + 1),
                    )
            rz = epi.tile([P, 2 * O], F32, name="rz", tag="rz")
            nc.scalar.activation(out=rz[:], in_=rz_ps[:], func=ACT.Sigmoid)
            rh = epi.tile([P, O], F32, name="rh", tag="rh")
            nc.vector.tensor_tensor(out=rh[:], in0=nn_ps[:, O : 2 * O], in1=rz[:, 0:O], op=ALU.mult)
            blend_first(u - 1)
            zp = epi.tile([P, O], F32, name="zp", tag="zp")
            nc.vector.tensor_tensor(out=zp[:], in0=rz[:, O : 2 * O], in1=h_sb[q][:, v * O : (v + 1) * O], op=ALU.mult)
            blend_second(u - 1)
            npre = epi.tile([P, O], F32, name="npre", tag="npre")
            nc.vector.tensor_tensor(out=npre[:], in0=nn_ps[:, 0:O], in1=rh[:], op=ALU.add)
            nt = epi.tile([P, O], F32, name="nt", tag="nt")
            nc.scalar.activation(out=nt[:], in_=npre[:], func=ACT.Tanh)
            pending[u] = (rz, zp, nt)

        def blend_first(u):
            if u >= 0:
                rz, zp, nt = pending[u]
                zn = epi.tile([P, O], F32, name="zn", tag="zn")
                nc.vector.scalar_tensor_tensor(
                    out=zn[:], in0=rz[:, O : 2 * O], scalar=1.0, in1=nt[:], op0=ALU.subtract, op1=ALU.mult
                )
                pending[u] = (zp, zn)

        def blend_second(u):
            if u >= 0:
                zp, zn = pending[u]
                res = epi.tile([P, O], F32, name="res", tag="res", align_bytes=256)
                nc.vector.tensor_tensor(out=res[:], in0=zp[:], in1=zn[:], op=ALU.subtract)
                nc.sync.dma_start(out=out[:, u, :], in_=res[:])

        def prep(q):
            weight_prep(q)
            pair_prep(q)
            weight_quantize(q)

        prep(0)
        prep(1)
        for q in range(PAIRS):
            unit(2 * q)
            unit(2 * q + 1)
            if q + 2 < PAIRS:
                prep(q + 2)
        blend_first(U - 1)
        blend_second(U - 1)
